import numpy as np
import ml_dtypes


def mxq(x, axis, fmt="e4m3"):
    dtype, down = {"e4m3": (ml_dtypes.float8_e4m3fn, 7), "e5m2": (ml_dtypes.float8_e5m2, 14)}[fmt]
    v = np.moveaxis(np.asarray(x, np.float32).astype(ml_dtypes.bfloat16).astype(np.float64), axis, -1)
    blocks = v.reshape(v.shape[:-1] + (-1, 32))
    amax = np.abs(blocks).max(-1, keepdims=True)
    byte = np.maximum(np.where(amax > 0, np.frexp(amax)[1] - 1 + 127, 0) - down, 1)
    scale = np.exp2(byte - 127.0)
    codes = (blocks / scale).astype(np.float32).astype(dtype).astype(np.float64)
    return np.moveaxis((codes * scale).reshape(v.shape), -1, axis)


WIDE = False


def mx_kscale(k):
    if not WIDE:
        return np.ones(k)
    levels = np.array([10, -10, 5, -5, 0])
    if k % 512:
        return np.exp2(np.random.permutation(np.resize(levels, k // 32))).repeat(32)
    a = np.empty((k // 512, 16))
    for p in range(k // 512):
        a[p, :8] = np.random.permutation(np.resize(levels, 8))
        for g in range(8):
            far = levels[np.abs(levels - a[p, g]) >= 10]
            a[p, g + 8] = far[np.random.randint(len(far))]
    return np.exp2(a.ravel()).repeat(32)


BF16 = ml_dtypes.bfloat16


def bf(x):
    return np.asarray(x, np.float32).astype(BF16)


def f64(x):
    return np.asarray(x).astype(np.float64)


B, L, E, H, DH, RK, RD, MAXLEN = 4, 1024, 512, 4, 64, 512, 128, 4096


def apply_rope(x, cos, sin):
    cos = cos[None, :, None, :]
    sin = sin[None, :, None, :]
    x1, x2 = x[..., 0::2], x[..., 1::2]
    out_real = x1 * cos - x2 * sin
    out_imag = x1 * sin + x2 * cos
    return np.stack([out_real, out_imag], axis=-1).reshape(x.shape)


def draw0():
    s, t = mx_kscale(E), mx_kscale(RK)
    tc = np.concatenate([t, np.ones(RD)])
    return {"x": bf(np.random.standard_normal((B, L, E)) * s),
            "cos": bf(np.random.uniform(size=(L, RD // 2))),
            "sin": bf(np.random.uniform(size=(L, RD // 2))),
            "wkv_down": bf(np.random.standard_normal((E, RK + RD)) / np.sqrt(E) / s[:, None] * tc),
            "w_up": bf(np.random.standard_normal((RK, H * (2 * DH + RD))) / np.sqrt(RK) / t[:, None])}


def core(x, cos, sin, wkv_down, w_up):
    kv_lat = mxq(f64(x), 2, "e4m3") @ mxq(f64(wkv_down), 0, "e4m3")
    c_kv = kv_lat[..., :RK]
    k_rope = kv_lat[..., RK:]
    k_rope = apply_rope(k_rope[:, :, None, :], f64(cos), f64(sin))[:, :, 0, :]
    up = (mxq(c_kv, 2, "e4m3") @ mxq(f64(w_up), 0, "e4m3")).reshape(B, L, H, 2 * DH + RD)
    k_head = up[..., :DH]
    v_head = up[..., DH:2 * DH]
    v_rope = up[..., 2 * DH:]
    k_rope_b = np.broadcast_to(k_rope[:, :, None, :], (B, L, H, RD))
    k = np.concatenate([k_head, k_rope_b], axis=-1)
    v = np.concatenate([v_head, v_rope], axis=-1)
    return k, v


def e4m3fn_bytes(y):
    return np.clip(np.asarray(y, np.float64), -448.0, 448.0).astype(np.float32).astype(ml_dtypes.float8_e4m3fn).view(np.uint8)


def e4m3fn_values(b):
    return np.asarray(b, np.uint8).view(ml_dtypes.float8_e4m3fn).astype(np.float64)


def setup_inputs():
    d = draw0()
    x0 = np.asarray(d['x']).astype(np.float64)
    s = (np.max(np.abs(x0), axis=(0, 1), keepdims=True) / 448.0).astype(np.float32)
    out = {}
    for k, v in d.items():
        if k == 'x':
            out['x_bytes'] = e4m3fn_bytes(x0 / s.astype(np.float64))
            out['x_scale'] = s
        else:
            out[k] = v
    return out


def reference(x_bytes, x_scale, cos, sin, wkv_down, w_up):
    return core(e4m3fn_values(x_bytes) * x_scale.astype(np.float64), cos, sin, wkv_down, w_up)

@@ -1,0 +1,301 @@
+from contextlib import ExitStack
+
+import concourse.mybir as mybir
+from concourse.masks import make_identity
+
+FLOPS = 2 * 4096 * 512 * 640 + 2 * 4096 * 512 * 1024
+
+F32 = mybir.dt.float32
+BF16 = mybir.dt.bfloat16
+U32 = mybir.dt.uint32
+U8 = mybir.dt.uint8
+FP8 = mybir.dt.float8_e4m3fn
+FP8X4 = mybir.dt.float8_e4m3fn_x4
+MULT = mybir.AluOpType.mult
+ADD = mybir.AluOpType.add
+
+P = 128
+STEPS = 16
+X_LOADS = ((0, 1), (1, 2), (2, 4), (4, 8))
+CAST_ON_SCALAR = (0, 1, 2)
+
+
+def tile_multiheadlatentattention_pa_t_kernel(tc, x_bytes, x_scale, cos, sin, wkv_down, w_up, out_0, out_1):
+    nc = tc.nc
+    x_view = x_bytes.rearrange("b l k -> (b l) k").rearrange("(g p i) k -> p g (i k)", p=P, i=4)
+    k_view = out_0.rearrange("b l h d -> (b l) (h d)").rearrange("(g p s i) c -> g s p (i c)", p=P, s=2, i=2)
+    v_view = out_1.rearrange("b l h d -> (b l) (h d)").rearrange("(g p s i) c -> g s p (i c)", p=P, s=2, i=2)
+
+    with ExitStack() as ctx:
+        keep = ctx.enter_context(tc.tile_pool(name="keep", bufs=1))
+        work = ctx.enter_context(tc.tile_pool(name="work", bufs=3))
+        psum = ctx.enter_context(tc.psum_pool(name="psum", bufs=1))
+        ctx.enter_context(tc.manual_schedule())
+
+        ident = keep.tile([P, P], F32, name="ident")
+        scale = keep.tile([P, 4], F32, name="scale")
+        w_raw = keep.tile([P, 4, 640], BF16, name="w_raw")
+        u_raw = keep.tile([P, 4, 1024], BF16, name="u_raw")
+        table = keep.tile([P, 2, 2, 256], BF16, name="table")
+        lat_g = keep.tile([P, 2048], BF16, name="lat_g", align_bytes=64)
+        rope_g = keep.tile([P, 1024], BF16, name="rope_g", align_bytes=64)
+        up_g = [keep.tile([P, 2048], BF16, name="up_g%d" % i, align_bytes=64) for i in range(2)]
+        lat_q = keep.tile([P, 512], U32, name="lat_q", align_bytes=64)
+        lat_s = keep.tile([P, 512], U8, name="lat_s", align_bytes=64)
+        rope_q = keep.tile([P, 256], U32, name="rope_q", align_bytes=64)
+        rope_s = keep.tile([P, 256], U8, name="rope_s", align_bytes=64)
+        up_q = [keep.tile([P, 512], U32, name="up_q%d" % i, align_bytes=64) for i in range(2)]
+        up_s = [keep.tile([P, 512], U8, name="up_s%d" % i, align_bytes=64) for i in range(2)]
+
+        make_identity(nc, ident[:])
+
+        x_raw = {}
+        for a, b in X_LOADS:
+            t = keep.tile([P, b - a, 2048], U8, name="x_raw%d" % a)
+            for g in range(a, b):
+                x_raw[g] = t[:, g - a, :]
+            if a == 1:
+                nc.sync.dma_start(out=w_raw[:], in_=wkv_down.rearrange("(p j) c -> p j c", j=4))
+                nc.sync.dma_start(out=u_raw[:], in_=w_up.rearrange("(p j) c -> p j c", j=4))
+                nc.sync.dma_start(out=table[:, 0, :, :], in_=cos.rearrange("(g p i) j -> p g (i j)", p=P, i=4))
+                nc.sync.dma_start(out=table[:, 1, :, :], in_=sin.rearrange("(g p i) j -> p g (i j)", p=P, i=4))
+            nc.sync.dma_start(out=t[:], in_=x_view[:, a:b, :])
+        nc.scalar.dma_start(out=scale[:], in_=x_scale.rearrange("a b (p t) -> p (a b t)", t=4))
+
+        x_bf, xt, xg, xq, xs, cb, rb, ub, cg, cq, cs, kv, rt = {}, {}, {}, {}, {}, {}, {}, {}, {}, {}, {}, {}, {}
+
+        def ok(n):
+            return 0 <= n < STEPS
+
+        def cast(n):
+            if not ok(n):
+                return
+            t = work.tile([P, 1024], BF16, name="x_bf")
+            x_bf[n] = t
+            s = n % 2
+            src = x_raw[n // 2][:, 1024 * s : 1024 * (s + 1)].bitcast(FP8)
+            if n in CAST_ON_SCALAR:
+                nc.scalar.copy(out=t[:], in_=src)
+            else:
+                nc.vector.tensor_copy(out=t[:], in_=src)
+
+        def turn(n):
+            if not ok(n):
+                return
+            t = psum.tile([P, 2, 2, 128], F32, name="xt")
+            xt[n] = t
+            words = x_bf[n][:].bitcast(F32)
+            for i in range(2):
+                for u in range(2):
+                    nc.tensor.transpose(t[:, u, i, :], words[:, 256 * i + u : 256 * (i + 1) : 2], ident[:])
+
+        def rescale(n):
+            if not ok(n):
+                return
+            t = work.tile([P, 1024], BF16, name="xg", align_bytes=64)
+            xg[n] = t
+            nc.vector.tensor_tensor(
+                out=t[:].rearrange("p (m u e) -> p m u e", u=2, e=2),
+                in0=xt[n][:].rearrange("p u i n -> p (u i n)").bitcast(BF16).rearrange("p (u m e) -> p m u e", u=2, e=2),
+                in1=scale[:].rearrange("p (u e) -> p u e", e=2).unsqueeze(1).to_broadcast([P, 256, 2, 2]),
+                op=MULT,
+            )
+
+        def quant(src, width, codes, scales):
+            nc.vector.quantize_mx(out=codes.bitcast(FP8X4), scales=scales, in_=src)
+
+        def quant_x(n):
+            if not ok(n):
+                return
+            q = work.tile([P, 256], U32, name="xq", align_bytes=64)
+            s = work.tile([P, 256], U8, name="xs", align_bytes=64)
+            xq[n], xs[n] = q, s
+            quant(xg[n][:], 1024, q[:], s[:])
+
+        def latent_mm(n):
+            if not ok(n):
+                return
+            for i in range(2):
+                t = psum.tile([P, 4, 128], F32, name="cb%d" % i)
+                cb[n, i] = t
+                for j in range(4):
+                    nc.tensor.matmul_mx(
+                        out=t[:, j, :],
+                        lhsT=lat_q[:, 128 * j : 128 * (j + 1)].bitcast(FP8X4),
+                        lhsT_scale=lat_s[:, 128 * j : 128 * (j + 1)],
+                        rhs=xq[n][:, 128 * i : 128 * (i + 1)].bitcast(FP8X4),
+                        rhs_scale=xs[n][:, 128 * i : 128 * (i + 1)],
+                        start=True,
+                        stop=True,
+                    )
+
+        def rope_mm(n):
+            if not ok(n):
+                return
+            t = psum.tile([P, 2, 256], F32, name="rb")
+            rb[n] = t
+            for i in range(2):
+                for a in range(2):
+                    nc.tensor.matmul_mx(
+                        out=t[:, a, 128 * i : 128 * (i + 1)],
+                        lhsT=xq[n][:, 128 * i : 128 * (i + 1)].bitcast(FP8X4),
+                        lhsT_scale=xs[n][:, 128 * i : 128 * (i + 1)],
+                        rhs=rope_q[:, 128 * a : 128 * (a + 1)].bitcast(FP8X4),
+                        rhs_scale=rope_s[:, 128 * a : 128 * (a + 1)],
+                        start=True,
+                        stop=True,
+                    )
+
+        def latent_out(n):
+            if not ok(n):
+                return
+            g = work.tile([P, 1024], BF16, name="cg", align_bytes=64)
+            cg[n] = g
+            for i in range(2):
+                nc.scalar.copy(
+                    out=g[:, 512 * i : 512 * (i + 1)].rearrange("p (n t) -> p n t", t=4),
+                    in_=cb[n, i][:].rearrange("p t n -> p n t"),
+                )
+
+        def quant_c(n):
+            if not ok(n):
+                return
+            q = work.tile([P, 256], U32, name="cq", align_bytes=64)
+            s = work.tile([P, 256], U8, name="cs", align_bytes=64)
+            cq[n], cs[n] = q, s
+            quant(cg[n][:], 1024, q[:], s[:])
+
+        def rope_mul(n):
+            if not ok(n):
+                return
+            t = work.tile([P, 2, 256], F32, name="rt")
+            rt[n] = t
+            g, s = (n // 2) % 2, n % 2
+            nc.vector.tensor_tensor(
+                out=t[:].rearrange("p a (m e) -> p a m e", e=2),
+                in0=rb[n][:].rearrange("p a (m e) -> p a m e", e=2),
+                in1=table[:, :, g, 128 * s : 128 * (s + 1)].unsqueeze(3).to_broadcast([P, 2, 128, 2]),
+                op=MULT,
+            )
+
+        def rope_add(n):
+            if not ok(n):
+                return
+            t = work.tile([P, 2, 2, 4, 192], F32, name="kv")
+            kv[n] = t
+            nc.vector.tensor_tensor(
+                out=t[:, 0, :, 0, 64:192],
+                in0=rt[n][:, 0, :].rearrange("p (i c) -> p i c", i=2),
+                in1=rt[n][:, 1, :].rearrange("p (i c) -> p i c", i=2),
+                op=ADD,
+            )
+
+        def rope_spread(n):
+            if not ok(n):
+                return
+            t = kv[n]
+            nc.vector.tensor_copy(
+                out=t[:, 0, :, 1:4, 64:192],
+                in_=t[:, 0, :, 0, 64:192].unsqueeze(2).to_broadcast([P, 2, 3, 128]),
+            )
+
+        def up_mm(n, i):
+            if not ok(n):
+                return
+            for half in range(2):
+                t = psum.tile([P, 512], F32, name="ub%d%d" % (i, half))
+                ub[n, i, half] = t
+                nc.tensor.matmul_mx(
+                    out=t[:],
+                    lhsT=cq[n][:, 128 * i : 128 * (i + 1)].bitcast(FP8X4),
+                    lhsT_scale=cs[n][:, 128 * i : 128 * (i + 1)],
+                    rhs=up_q[half][:].bitcast(FP8X4),
+                    rhs_scale=up_s[half][:],
+                    start=True,
+                    stop=True,
+                )
+
+        def up_out(n, i):
+            if not ok(n):
+                return
+            nc.scalar.copy(
+                out=kv[n][:, :, i, :, 0:64].rearrange("p a h c -> p h a c"),
+                in_=ub[n, i, 0][:].rearrange("p (h a c) -> p h a c", h=4, a=2),
+            )
+            nc.scalar.copy(
+                out=kv[n][:, 1, i, :, 64:192],
+                in_=ub[n, i, 1][:].rearrange("p (h c) -> p h c", h=4),
+            )
+
+        def store(n):
+            if not ok(n):
+                return
+            g, s = n // 2, n % 2
+            nc.sync.dma_start(out=k_view[g, s], in_=kv[n][:, 0].rearrange("p i h d -> p (i h d)"))
+            nc.sync.dma_start(out=v_view[g, s], in_=kv[n][:, 1].rearrange("p i h d -> p (i h d)"))
+
+        lat_out_view = lat_g[:].rearrange("p (t m j) -> p t m j", t=4, j=4)
+        lat_in_view = w_raw[:, :, 0:512].rearrange("p j (m t) -> p t m j", t=4)
+        rope_out_view = rope_g[:].rearrange("p (a c j) -> p a c j", a=2, j=4)
+        rope_in_view = w_raw[:, :, 512:640].rearrange("p j c -> p c j")
+        up_in_view = u_raw[:].rearrange("p j (h f c) -> p f h c j", h=4, f=2)
+
+        cast(0)
+        turn(0)
+        cast(1)
+        nc.scalar.copy(out=lat_out_view[:, 2:4], in_=lat_in_view[:, 2:4])
+        nc.scalar.copy(out=rope_out_view[:, 0], in_=rope_in_view)
+        nc.scalar.copy(out=rope_out_view[:, 1, 1::2], in_=rope_in_view[:, 0::2])
+        rescale(0)
+        nc.vector.tensor_copy(out=lat_out_view[:, 0:2], in_=lat_in_view[:, 0:2])
+        quant_x(0)
+        nc.vector.tensor_scalar(out=rope_out_view[:, 1, 0::2], in0=rope_in_view[:, 1::2], scalar1=-1.0, scalar2=None, op0=MULT)
+        quant(lat_g[:], 2048, lat_q[:], lat_s[:])
+        turn(1)
+        latent_mm(0)
+        quant(rope_g[:], 1024, rope_q[:], rope_s[:])
+        rope_mm(0)
+        cast(2)
+        latent_out(0)
+        for f, h in ((0, 0), (0, 2), (1, 0)):
+            nc.vector.tensor_copy(
+                out=up_g[f][:].rearrange("p (h c j) -> p h c j", h=4, j=4)[:, h : h + 2],
+                in_=up_in_view[:, f, h : h + 2],
+            )
+            if f == 0 and h == 2:
+                quant_c(0)
+                quant(up_g[0][:], 2048, up_q[0][:], up_s[0][:])
+                rescale(1)
+        nc.scalar.copy(
+            out=up_g[1][:].rearrange("p (h c j) -> p h c j", h=4, j=4)[:, 2:4],
+            in_=up_in_view[:, 1, 2:4],
+        )
+        quant_x(1)
+        quant(up_g[1][:], 2048, up_q[1][:], up_s[1][:])
+        turn(2)
+        latent_mm(1)
+        up_mm(0, 0)
+        rope_mul(0)
+        rope_mm(1)
+        rope_add(0)
+        cast(3)
+        rope_spread(0)
+        up_mm(0, 1)
+
+        for n in range(STEPS):
+            latent_out(n + 1)
+            rescale(n + 2)
+            quant_c(n + 1)
+            turn(n + 3)
+            rope_mul(n + 1)
+            quant_x(n + 2)
+            latent_mm(n + 2)
+            up_out(n, 0)
+            up_mm(n + 1, 0)
+            rope_mm(n + 2)
+            rope_add(n + 1)
+            cast(n + 4)
+            up_out(n, 1)
+            rope_spread(n + 1)
+            store(n)
+            up_mm(n + 1, 1)

@@ -16,13 +16,13 @@ ADD = mybir.AluOpType.add
 
 P = 128
 STEPS = 16
-X_LOADS = ((0, 1), (1, 2), (2, 4), (4, 8))
-CAST_ON_SCALAR = (0, 1, 2)
+CAST_ON_SCALAR = (2,)
 
 
 def tile_multiheadlatentattention_pa_t_kernel(tc, x_bytes, x_scale, cos, sin, wkv_down, w_up, out_0, out_1):
     nc = tc.nc
-    x_view = x_bytes.rearrange("b l k -> (b l) k").rearrange("(g p i) k -> p g (i k)", p=P, i=4)
+    x_view = x_bytes.rearrange("b l k -> (b l) k").rearrange("(g p s i) k -> g s p (i k)", p=P, s=2, i=2)
+    x_whole = x_bytes.rearrange("b l k -> (b l) k").rearrange("(g p i) k -> p g (i k)", p=P, i=4)
     k_view = out_0.rearrange("b l h d -> (b l) (h d)").rearrange("(g p s i) c -> g s p (i c)", p=P, s=2, i=2)
     v_view = out_1.rearrange("b l h d -> (b l) (h d)").rearrange("(g p s i) c -> g s p (i c)", p=P, s=2, i=2)
 
@@ -49,18 +49,28 @@ def tile_multiheadlatentattention_pa_t_kernel(tc, x_bytes, x_scale, cos, sin, wk
 
         make_identity(nc, ident[:])
 
-        x_raw = {}
-        for a, b in X_LOADS:
-            t = keep.tile([P, b - a, 2048], U8, name="x_raw%d" % a)
-            for g in range(a, b):
-                x_raw[g] = t[:, g - a, :]
-            if a == 1:
-                nc.sync.dma_start(out=w_raw[:], in_=wkv_down.rearrange("(p j) c -> p j c", j=4))
-                nc.sync.dma_start(out=u_raw[:], in_=w_up.rearrange("(p j) c -> p j c", j=4))
-                nc.sync.dma_start(out=table[:, 0, :, :], in_=cos.rearrange("(g p i) j -> p g (i j)", p=P, i=4))
-                nc.sync.dma_start(out=table[:, 1, :, :], in_=sin.rearrange("(g p i) j -> p g (i j)", p=P, i=4))
-            nc.sync.dma_start(out=t[:], in_=x_view[:, a:b, :])
         nc.scalar.dma_start(out=scale[:], in_=x_scale.rearrange("a b (p t) -> p (a b t)", t=4))
+
+        x_raw = {}
+
+        def load_x(a, b):
+            t = keep.tile([P, b - a, 1024], U8, name="x_raw%d" % a)
+            for n in range(a, b):
+                x_raw[n] = t[:, n - a, :]
+            if b - a == 1:
+                nc.sync.dma_start(out=t[:, 0, :], in_=x_view[a // 2, a % 2])
+            else:
+                nc.sync.dma_start(out=t[:].rearrange("p (g c) k -> p g (c k)", c=2), in_=x_whole[:, a // 2 : b // 2, :])
+
+        load_x(0, 1)
+        load_x(1, 2)
+        nc.sync.dma_start(out=w_raw[:], in_=wkv_down.rearrange("(p j) c -> p j c", j=4))
+        nc.sync.dma_start(out=u_raw[:], in_=w_up.rearrange("(p j) c -> p j c", j=4))
+        load_x(2, 4)
+        nc.sync.dma_start(out=table[:, 0, :, :], in_=cos.rearrange("(g p i) j -> p g (i j)", p=P, i=4))
+        nc.sync.dma_start(out=table[:, 1, :, :], in_=sin.rearrange("(g p i) j -> p g (i j)", p=P, i=4))
+        load_x(4, 8)
+        load_x(8, 16)
 
         x_bf, xt, xg, xq, xs, cb, rb, ub, cg, cq, cs, kv, rt = {}, {}, {}, {}, {}, {}, {}, {}, {}, {}, {}, {}, {}
 
@@ -72,8 +82,7 @@ def tile_multiheadlatentattention_pa_t_kernel(tc, x_bytes, x_scale, cos, sin, wk
                 return
             t = work.tile([P, 1024], BF16, name="x_bf")
             x_bf[n] = t
-            s = n % 2
-            src = x_raw[n // 2][:, 1024 * s : 1024 * (s + 1)].bitcast(FP8)
+            src = x_raw[n].bitcast(FP8)
             if n in CAST_ON_SCALAR:
                 nc.scalar.copy(out=t[:], in_=src)
             else:
@@ -178,11 +187,15 @@ def tile_multiheadlatentattention_pa_t_kernel(tc, x_bytes, x_scale, cos, sin, wk
                 op=MULT,
             )
 
+        def kv_tile(n):
+            if n not in kv:
+                kv[n] = work.tile([P, 2, 2, 4, 192], F32, name="kv", bufs=6)
+            return kv[n]
+
         def rope_add(n):
             if not ok(n):
                 return
-            t = work.tile([P, 2, 2, 4, 192], F32, name="kv")
-            kv[n] = t
+            t = kv_tile(n)
             nc.vector.tensor_tensor(
                 out=t[:, 0, :, 0, 64:192],
                 in0=rt[n][:, 0, :].rearrange("p (i c) -> p i c", i=2),
@@ -194,15 +207,19 @@ def tile_multiheadlatentattention_pa_t_kernel(tc, x_bytes, x_scale, cos, sin, wk
             if not ok(n):
                 return
             t = kv[n]
-            nc.vector.tensor_copy(
+            nc.gpsimd.tensor_scalar(
                 out=t[:, 0, :, 1:4, 64:192],
-                in_=t[:, 0, :, 0, 64:192].unsqueeze(2).to_broadcast([P, 2, 3, 128]),
+                in0=t[:, 0, :, 0, 64:192].unsqueeze(2).to_broadcast([P, 2, 3, 128]),
+                scalar1=1.0,
+                scalar2=0.0,
+                op0=MULT,
+                op1=ADD,
             )
 
-        def up_mm(n, i):
+        def up_mm(n, i, halves=(0, 1)):
             if not ok(n):
                 return
-            for half in range(2):
+            for half in halves:
                 t = psum.tile([P, 512], F32, name="ub%d%d" % (i, half))
                 ub[n, i, half] = t
                 nc.tensor.matmul_mx(
@@ -215,24 +232,29 @@ def tile_multiheadlatentattention_pa_t_kernel(tc, x_bytes, x_scale, cos, sin, wk
                     stop=True,
                 )
 
-        def up_out(n, i):
+        def up_out(n, i, halves=(0, 1), copy=nc.scalar.copy):
             if not ok(n):
                 return
-            nc.scalar.copy(
-                out=kv[n][:, :, i, :, 0:64].rearrange("p a h c -> p h a c"),
-                in_=ub[n, i, 0][:].rearrange("p (h a c) -> p h a c", h=4, a=2),
-            )
-            nc.scalar.copy(
-                out=kv[n][:, 1, i, :, 64:192],
-                in_=ub[n, i, 1][:].rearrange("p (h c) -> p h c", h=4),
-            )
+            for half in halves:
+                if half == 0:
+                    copy(
+                        out=kv_tile(n)[:, :, i, :, 0:64].rearrange("p a h c -> p h a c"),
+                        in_=ub[n, i, 0][:].rearrange("p (h a c) -> p h a c", h=4, a=2),
+                    )
+                else:
+                    copy(
+                        out=kv_tile(n)[:, 1, i, :, 64:192],
+                        in_=ub[n, i, 1][:].rearrange("p (h c) -> p h c", h=4),
+                    )
 
-        def store(n):
+        def store(n, i=None):
             if not ok(n):
                 return
             g, s = n // 2, n % 2
-            nc.sync.dma_start(out=k_view[g, s], in_=kv[n][:, 0].rearrange("p i h d -> p (i h d)"))
-            nc.sync.dma_start(out=v_view[g, s], in_=kv[n][:, 1].rearrange("p i h d -> p (i h d)"))
+            a, b = (0, 2) if i is None else (i, i + 1)
+            for once in range(1):
+                nc.sync.dma_start(out=k_view[g, s][:, 768 * a : 768 * b], in_=kv[n][:, 0, a:b].rearrange("p i h d -> p (i h d)"))
+                nc.sync.dma_start(out=v_view[g, s][:, 768 * a : 768 * b], in_=kv[n][:, 1, a:b].rearrange("p i h d -> p (i h d)"))
 
         lat_out_view = lat_g[:].rearrange("p (t m j) -> p t m j", t=4, j=4)
         lat_in_view = w_raw[:, :, 0:512].rearrange("p j (m t) -> p t m j", t=4)
@@ -240,62 +262,330 @@ def tile_multiheadlatentattention_pa_t_kernel(tc, x_bytes, x_scale, cos, sin, wk
         rope_in_view = w_raw[:, :, 512:640].rearrange("p j c -> p c j")
         up_in_view = u_raw[:].rearrange("p j (h f c) -> p f h c j", h=4, f=2)
 
+        def lat_copy(a, b, copy):
+            copy(out=lat_out_view[:, a:b], in_=lat_in_view[:, a:b])
+
+        def rope_copy(kind):
+            if kind == 0:
+                nc.scalar.copy(out=rope_out_view[:, 0], in_=rope_in_view)
+            elif kind == 1:
+                nc.scalar.copy(out=rope_out_view[:, 1, 1::2], in_=rope_in_view[:, 0::2])
+            else:
+                nc.vector.tensor_scalar(out=rope_out_view[:, 1, 0::2], in0=rope_in_view[:, 1::2], scalar1=-1.0, scalar2=None, op0=MULT)
+
+        def quant_lat():
+            quant(lat_g[:], 2048, lat_q[:], lat_s[:])
+
+        def quant_rope():
+            quant(rope_g[:], 1024, rope_q[:], rope_s[:])
+
+        def quant_up(f):
+            quant(up_g[f][:], 2048, up_q[f][:], up_s[f][:])
+
+        def up_group(f, h, h_end, copy):
+            copy(
+                out=up_g[f][:].rearrange("p (h c j) -> p h c j", h=4, j=4)[:, h:h_end],
+                in_=up_in_view[:, f, h:h_end],
+            )
+
         cast(0)
         turn(0)
         cast(1)
-        nc.scalar.copy(out=lat_out_view[:, 2:4], in_=lat_in_view[:, 2:4])
-        nc.scalar.copy(out=rope_out_view[:, 0], in_=rope_in_view)
-        nc.scalar.copy(out=rope_out_view[:, 1, 1::2], in_=rope_in_view[:, 0::2])
+        rope_copy(2)
+        rope_copy(0)
+        rope_copy(1)
+        lat_copy(1, 4, nc.scalar.copy)
         rescale(0)
-        nc.vector.tensor_copy(out=lat_out_view[:, 0:2], in_=lat_in_view[:, 0:2])
-        quant_x(0)
-        nc.vector.tensor_scalar(out=rope_out_view[:, 1, 0::2], in0=rope_in_view[:, 1::2], scalar1=-1.0, scalar2=None, op0=MULT)
-        quant(lat_g[:], 2048, lat_q[:], lat_s[:])
         turn(1)
-        latent_mm(0)
-        quant(rope_g[:], 1024, rope_q[:], rope_s[:])
+        lat_copy(0, 1, nc.vector.tensor_copy)
+        quant_rope()
+        quant_x(0)
         rope_mm(0)
+        up_group(0, 0, 4, nc.vector.tensor_copy)
+        quant_lat()
+        latent_mm(0)
         cast(2)
         latent_out(0)
-        for f, h in ((0, 0), (0, 2), (1, 0)):
-            nc.vector.tensor_copy(
-                out=up_g[f][:].rearrange("p (h c j) -> p h c j", h=4, j=4)[:, h : h + 2],
-                in_=up_in_view[:, f, h : h + 2],
-            )
-            if f == 0 and h == 2:
-                quant_c(0)
-                quant(up_g[0][:], 2048, up_q[0][:], up_s[0][:])
-                rescale(1)
-        nc.scalar.copy(
-            out=up_g[1][:].rearrange("p (h c j) -> p h c j", h=4, j=4)[:, 2:4],
-            in_=up_in_view[:, 1, 2:4],
-        )
-        quant_x(1)
-        quant(up_g[1][:], 2048, up_q[1][:], up_s[1][:])
-        turn(2)
-        latent_mm(1)
-        up_mm(0, 0)
+        quant_up(0)
         rope_mul(0)
-        rope_mm(1)
-        rope_add(0)
+        rescale(1)
+        turn(2)
+        up_group(1, 0, 2, nc.scalar.copy)
+        up_group(1, 2, 4, nc.vector.tensor_copy)
         cast(3)
+        quant_x(1)
+        latent_mm(1)
+        quant_c(0)
+        up_mm(0, 0, (0,))
+        up_mm(0, 1, (0,))
+        rescale(2)
+        turn(3)
+        latent_out(1)
+        quant_up(1)
+        up_mm(0, 0, (1,))
+        up_mm(0, 1, (1,))
+        rope_mm(1)
+        quant_x(2)
+        latent_mm(2)
+        up_out(0, 0)
+        rope_add(0)
         rope_spread(0)
-        up_mm(0, 1)
-
-        for n in range(STEPS):
-            latent_out(n + 1)
-            rescale(n + 2)
-            quant_c(n + 1)
-            turn(n + 3)
-            rope_mul(n + 1)
-            quant_x(n + 2)
-            latent_mm(n + 2)
-            up_out(n, 0)
-            up_mm(n + 1, 0)
-            rope_mm(n + 2)
-            rope_add(n + 1)
-            cast(n + 4)
-            up_out(n, 1)
-            rope_spread(n + 1)
-            store(n)
-            up_mm(n + 1, 1)
+        store(0, 0)
+        up_out(0, 1)
+        store(0, 1)
+        quant_c(1)
+        up_mm(1, 0)
+        up_mm(1, 1)
+        rope_mul(1)
+        rope_mm(2)
+        cast(4)
+        latent_out(2)
+        rope_add(1)
+        rope_spread(1)
+        rescale(3)
+        turn(4)
+        up_out(1, 1, (1,), nc.vector.tensor_copy)
+        quant_c(2)
+        quant_x(3)
+        latent_mm(3)
+        up_out(1, 0)
+        up_mm(2, 0)
+        rope_mul(2)
+        rope_mm(3)
+        cast(5)
+        up_out(1, 1, (0,))
+        store(1)
+        up_mm(2, 1)
+        rope_add(2)
+        rope_spread(2)
+        latent_out(3)
+        rescale(4)
+        turn(5)
+        quant_c(3)
+        quant_x(4)
+        latent_mm(4)
+        up_out(2, 0)
+        up_mm(3, 0)
+        rope_mul(3)
+        rope_mm(4)
+        cast(6)
+        up_out(2, 1, (0, 1))
+        store(2)
+        up_mm(3, 1)
+        rope_add(3)
+        rope_spread(3)
+        latent_out(4)
+        rescale(5)
+        turn(6)
+        quant_c(4)
+        quant_x(5)
+        latent_mm(5)
+        up_out(3, 0)
+        up_mm(4, 0)
+        rope_mul(4)
+        rope_mm(5)
+        cast(7)
+        up_out(3, 1, (0, 1))
+        store(3)
+        up_mm(4, 1)
+        rope_add(4)
+        rope_spread(4)
+        latent_out(5)
+        rescale(6)
+        turn(7)
+        up_out(4, 1, (1,), nc.vector.tensor_copy)
+        quant_c(5)
+        quant_x(6)
+        latent_mm(6)
+        up_out(4, 0)
+        up_mm(5, 0)
+        rope_mul(5)
+        rope_mm(6)
+        cast(8)
+        up_out(4, 1, (0,))
+        store(4)
+        up_mm(5, 1)
+        rope_add(5)
+        rope_spread(5)
+        latent_out(6)
+        rescale(7)
+        turn(8)
+        quant_c(6)
+        quant_x(7)
+        latent_mm(7)
+        up_out(5, 0)
+        up_mm(6, 0)
+        rope_mul(6)
+        rope_mm(7)
+        cast(9)
+        up_out(5, 1, (0, 1))
+        store(5)
+        up_mm(6, 1)
+        rope_add(6)
+        rope_spread(6)
+        latent_out(7)
+        rescale(8)
+        turn(9)
+        quant_c(7)
+        quant_x(8)
+        latent_mm(8)
+        up_out(6, 0)
+        up_mm(7, 0)
+        rope_mul(7)
+        rope_mm(8)
+        cast(10)
+        up_out(6, 1, (0, 1))
+        store(6)
+        up_mm(7, 1)
+        rope_add(7)
+        rope_spread(7)
+        latent_out(8)
+        rescale(9)
+        turn(10)
+        up_out(7, 1, (1,), nc.vector.tensor_copy)
+        quant_c(8)
+        quant_x(9)
+        latent_mm(9)
+        up_out(7, 0)
+        up_mm(8, 0)
+        rope_mul(8)
+        rope_mm(9)
+        cast(11)
+        up_out(7, 1, (0,))
+        store(7)
+        up_mm(8, 1)
+        rope_add(8)
+        rope_spread(8)
+        latent_out(9)
+        rescale(10)
+        turn(11)
+        quant_c(9)
+        quant_x(10)
+        latent_mm(10)
+        up_out(8, 0)
+        up_mm(9, 0)
+        rope_mul(9)
+        rope_mm(10)
+        cast(12)
+        up_out(8, 1, (0, 1))
+        store(8)
+        up_mm(9, 1)
+        rope_add(9)
+        rope_spread(9)
+        latent_out(10)
+        rescale(11)
+        turn(12)
+        quant_c(10)
+        quant_x(11)
+        latent_mm(11)
+        up_out(9, 0)
+        up_mm(10, 0)
+        rope_mul(10)
+        rope_mm(11)
+        cast(13)
+        up_out(9, 1, (0, 1))
+        store(9)
+        up_mm(10, 1)
+        rope_add(10)
+        rope_spread(10)
+        latent_out(11)
+        rescale(12)
+        turn(13)
+        up_out(10, 1, (1,), nc.vector.tensor_copy)
+        quant_c(11)
+        quant_x(12)
+        latent_mm(12)
+        up_out(10, 0)
+        up_mm(11, 0)
+        rope_mul(11)
+        rope_mm(12)
+        cast(14)
+        up_out(10, 1, (0,))
+        store(10)
+        up_mm(11, 1)
+        rope_add(11)
+        rope_spread(11)
+        latent_out(12)
+        rescale(13)
+        turn(14)
+        quant_c(12)
+        quant_x(13)
+        latent_mm(13)
+        up_out(11, 0)
+        up_mm(12, 0)
+        rope_mul(12)
+        rope_mm(13)
+        cast(15)
+        up_out(11, 1, (0, 1))
+        store(11)
+        up_mm(12, 1)
+        rope_add(12)
+        rope_spread(12)
+        latent_out(13)
+        rescale(14)
+        turn(15)
+        quant_c(13)
+        quant_x(14)
+        latent_mm(14)
+        up_out(12, 0)
+        up_mm(13, 0)
+        rope_mul(13)
+        rope_mm(14)
+        cast(16)
+        up_out(12, 1, (0, 1))
+        store(12)
+        up_mm(13, 1)
+        rope_add(13)
+        rope_spread(13)
+        latent_out(14)
+        rescale(15)
+        turn(16)
+        up_out(13, 1, (1,), nc.vector.tensor_copy)
+        quant_c(14)
+        quant_x(15)
+        latent_mm(15)
+        up_out(13, 0)
+        up_mm(14, 0)
+        rope_mul(14)
+        rope_mm(15)
+        cast(17)
+        up_out(13, 1, (0,))
+        store(13)
+        up_mm(14, 1)
+        rope_add(14)
+        rope_spread(14)
+        latent_out(15)
+        rescale(16)
+        turn(17)
+        quant_c(15)
+        quant_x(16)
+        latent_mm(16)
+        up_out(14, 0)
+        store(14, 0)
+        up_mm(15, 0)
+        rope_mul(15)
+        rope_mm(16)
+        cast(18)
+        up_out(14, 1, (0, 1), nc.vector.tensor_copy)
+        store(14, 1)
+        up_mm(15, 1)
+        rope_add(15)
+        rope_spread(15)
+        latent_out(16)
+        rescale(17)
+        turn(18)
+        quant_c(16)
+        quant_x(17)
+        latent_mm(17)
+        up_out(15, 0)
+        store(15, 0)
+        up_mm(16, 0)
+        rope_mul(16)
+        rope_mm(17)
+        cast(19)
+        up_out(15, 1, (0, 1), nc.vector.tensor_copy)
+        store(15, 1)
+        up_mm(16, 1)
+        rope_add(16)
+        rope_spread(16)
+        latent_out(17)

@@ -247,14 +247,21 @@ def tile_multiheadlatentattention_pa_t_kernel(tc, x_bytes, x_scale, cos, sin, wk
                         in_=ub[n, i, 1][:].rearrange("p (h c) -> p h c", h=4),
                     )
 
+        def store_part(n, i, part):
+            if not ok(n):
+                return
+            g, s = n // 2, n % 2
+            view = k_view if part == 0 else v_view
+            nc.sync.dma_start(out=view[g, s][:, 768 * i : 768 * (i + 1)], in_=kv[n][:, part, i].rearrange("p h d -> p (h d)"))
+
         def store(n, i=None):
             if not ok(n):
                 return
             g, s = n // 2, n % 2
             a, b = (0, 2) if i is None else (i, i + 1)
             for once in range(1):
-                nc.sync.dma_start(out=k_view[g, s][:, 768 * a : 768 * b], in_=kv[n][:, 0, a:b].rearrange("p i h d -> p (i h d)"))
                 nc.sync.dma_start(out=v_view[g, s][:, 768 * a : 768 * b], in_=kv[n][:, 1, a:b].rearrange("p i h d -> p (i h d)"))
+                nc.sync.dma_start(out=k_view[g, s][:, 768 * a : 768 * b], in_=kv[n][:, 0, a:b].rearrange("p i h d -> p (i h d)"))
 
         lat_out_view = lat_g[:].rearrange("p (t m j) -> p t m j", t=4, j=4)
         lat_in_view = w_raw[:, :, 0:512].rearrange("p j (m t) -> p t m j", t=4)
@@ -289,303 +296,306 @@ def tile_multiheadlatentattention_pa_t_kernel(tc, x_bytes, x_scale, cos, sin, wk
             )
 
         cast(0)
-        turn(0)
+        rope_copy(1)
         cast(1)
         rope_copy(2)
         rope_copy(0)
-        rope_copy(1)
         lat_copy(1, 4, nc.scalar.copy)
+        turn(0)
         rescale(0)
-        turn(1)
         lat_copy(0, 1, nc.vector.tensor_copy)
         quant_rope()
         quant_x(0)
-        rope_mm(0)
-        up_group(0, 0, 4, nc.vector.tensor_copy)
-        quant_lat()
-        latent_mm(0)
+        turn(1)
         cast(2)
+        up_group(1, 2, 4, nc.vector.tensor_copy)
+        up_group(1, 0, 2, nc.scalar.copy)
+        rescale(1)
+        quant_lat()
+        quant_x(1)
+        rope_mm(0)
+        latent_mm(0)
+        turn(2)
+        up_group(0, 0, 4, nc.vector.tensor_copy)
+        rope_mul(0)
         latent_out(0)
         quant_up(0)
-        rope_mul(0)
-        rescale(1)
-        turn(2)
-        up_group(1, 0, 2, nc.scalar.copy)
-        up_group(1, 2, 4, nc.vector.tensor_copy)
-        cast(3)
-        quant_x(1)
-        latent_mm(1)
         quant_c(0)
-        up_mm(0, 0, (0,))
+        latent_mm(1)
+        cast(3)
+        latent_out(1)
         up_mm(0, 1, (0,))
+        up_mm(0, 0, (0,))
+        quant_up(1)
+        up_out(0, 0, (0,))
+        rope_mm(1)
+        up_mm(0, 0, (1,))
+        up_out(0, 0, (1,))
         rescale(2)
         turn(3)
-        latent_out(1)
-        quant_up(1)
-        up_mm(0, 0, (1,))
+        up_out(0, 1, (0,))
+        rope_mul(1)
+        rope_add(0)
         up_mm(0, 1, (1,))
-        rope_mm(1)
+        quant_c(1)
+        up_out(0, 1, (1,))
         quant_x(2)
         latent_mm(2)
-        up_out(0, 0)
-        rope_add(0)
-        rope_spread(0)
-        store(0, 0)
-        up_out(0, 1)
-        store(0, 1)
-        quant_c(1)
-        up_mm(1, 0)
-        up_mm(1, 1)
-        rope_mul(1)
-        rope_mm(2)
         cast(4)
+        store_part(0, 0, 1)
+        store_part(0, 1, 1)
+        rope_mm(2)
         latent_out(2)
         rope_add(1)
-        rope_spread(1)
+        rope_spread(0)
+        store_part(0, 0, 0)
+        up_mm(1, 1)
+        up_mm(1, 0)
+        up_out(1, 1, (0, 1))
         rescale(3)
-        turn(4)
-        up_out(1, 1, (1,), nc.vector.tensor_copy)
-        quant_c(2)
-        quant_x(3)
-        latent_mm(3)
-        up_out(1, 0)
-        up_mm(2, 0)
         rope_mul(2)
-        rope_mm(3)
-        cast(5)
-        up_out(1, 1, (0,))
-        store(1)
-        up_mm(2, 1)
+        turn(4)
+        quant_c(2)
+        store_part(0, 1, 0)
         rope_add(2)
-        rope_spread(2)
-        latent_out(3)
+        up_out(1, 0)
+        quant_x(3)
         rescale(4)
+        store_part(1, 1, 1)
+        rope_spread(1)
+        up_mm(2, 1)
+        cast(5)
+        store_part(1, 0, 0)
+        latent_mm(3)
+        up_mm(2, 0)
+        rope_mm(3)
+        store_part(1, 1, 0)
         turn(5)
-        quant_c(3)
-        quant_x(4)
-        latent_mm(4)
-        up_out(2, 0)
-        up_mm(3, 0)
+        store_part(1, 0, 1)
+        rope_spread(2)
+        up_out(2, 1, (1,), nc.vector.tensor_copy)
         rope_mul(3)
+        quant_x(4)
+        latent_out(3)
+        quant_c(3)
+        latent_mm(4)
         rope_mm(4)
         cast(6)
-        up_out(2, 1, (0, 1))
+        up_out(2, 0)
+        up_mm(3, 0)
+        up_out(2, 1, (0,))
         store(2)
         up_mm(3, 1)
         rope_add(3)
         rope_spread(3)
-        latent_out(4)
         rescale(5)
         turn(6)
-        quant_c(4)
-        quant_x(5)
-        latent_mm(5)
-        up_out(3, 0)
-        up_mm(4, 0)
         rope_mul(4)
+        quant_x(5)
+        latent_out(4)
+        quant_c(4)
+        latent_mm(5)
         rope_mm(5)
         cast(7)
+        up_out(3, 0)
+        up_mm(4, 0)
         up_out(3, 1, (0, 1))
         store(3)
         up_mm(4, 1)
         rope_add(4)
         rope_spread(4)
-        latent_out(5)
         rescale(6)
         turn(7)
-        up_out(4, 1, (1,), nc.vector.tensor_copy)
-        quant_c(5)
-        quant_x(6)
-        latent_mm(6)
-        up_out(4, 0)
-        up_mm(5, 0)
         rope_mul(5)
+        quant_x(6)
+        latent_out(5)
+        quant_c(5)
+        latent_mm(6)
         rope_mm(6)
         cast(8)
-        up_out(4, 1, (0,))
+        up_out(4, 0)
+        up_mm(5, 0)
+        up_out(4, 1, (0, 1))
         store(4)
         up_mm(5, 1)
         rope_add(5)
         rope_spread(5)
-        latent_out(6)
         rescale(7)
         turn(8)
-        quant_c(6)
-        quant_x(7)
-        latent_mm(7)
-        up_out(5, 0)
-        up_mm(6, 0)
         rope_mul(6)
+        up_out(5, 1, (1,), nc.vector.tensor_copy)
+        quant_x(7)
+        latent_out(6)
+        quant_c(6)
+        latent_mm(7)
         rope_mm(7)
         cast(9)
-        up_out(5, 1, (0, 1))
+        up_out(5, 0)
+        up_mm(6, 0)
+        up_out(5, 1, (0,))
         store(5)
         up_mm(6, 1)
         rope_add(6)
         rope_spread(6)
-        latent_out(7)
         rescale(8)
         turn(9)
-        quant_c(7)
-        quant_x(8)
-        latent_mm(8)
-        up_out(6, 0)
-        up_mm(7, 0)
         rope_mul(7)
+        quant_x(8)
+        latent_out(7)
+        quant_c(7)
+        latent_mm(8)
         rope_mm(8)
         cast(10)
+        up_out(6, 0)
+        up_mm(7, 0)
         up_out(6, 1, (0, 1))
         store(6)
         up_mm(7, 1)
         rope_add(7)
         rope_spread(7)
-        latent_out(8)
         rescale(9)
         turn(10)
-        up_out(7, 1, (1,), nc.vector.tensor_copy)
-        quant_c(8)
-        quant_x(9)
-        latent_mm(9)
-        up_out(7, 0)
-        up_mm(8, 0)
         rope_mul(8)
+        quant_x(9)
+        latent_out(8)
+        quant_c(8)
+        latent_mm(9)
         rope_mm(9)
         cast(11)
-        up_out(7, 1, (0,))
+        up_out(7, 0)
+        up_mm(8, 0)
+        up_out(7, 1, (0, 1))
         store(7)
         up_mm(8, 1)
         rope_add(8)
         rope_spread(8)
-        latent_out(9)
         rescale(10)
         turn(11)
-        quant_c(9)
-        quant_x(10)
-        latent_mm(10)
-        up_out(8, 0)
-        up_mm(9, 0)
         rope_mul(9)
+        up_out(8, 1, (1,), nc.vector.tensor_copy)
+        quant_x(10)
+        latent_out(9)
+        quant_c(9)
+        latent_mm(10)
         rope_mm(10)
         cast(12)
-        up_out(8, 1, (0, 1))
+        up_out(8, 0)
+        up_mm(9, 0)
+        up_out(8, 1, (0,))
         store(8)
         up_mm(9, 1)
         rope_add(9)
         rope_spread(9)
-        latent_out(10)
         rescale(11)
         turn(12)
-        quant_c(10)
-        quant_x(11)
-        latent_mm(11)
-        up_out(9, 0)
-        up_mm(10, 0)
         rope_mul(10)
+        quant_x(11)
+        latent_out(10)
+        quant_c(10)
+        latent_mm(11)
         rope_mm(11)
         cast(13)
+        up_out(9, 0)
+        up_mm(10, 0)
         up_out(9, 1, (0, 1))
         store(9)
         up_mm(10, 1)
         rope_add(10)
         rope_spread(10)
-        latent_out(11)
         rescale(12)
         turn(13)
-        up_out(10, 1, (1,), nc.vector.tensor_copy)
-        quant_c(11)
-        quant_x(12)
-        latent_mm(12)
-        up_out(10, 0)
-        up_mm(11, 0)
         rope_mul(11)
+        quant_x(12)
+        latent_out(11)
+        quant_c(11)
+        latent_mm(12)
         rope_mm(12)
         cast(14)
-        up_out(10, 1, (0,))
+        up_out(10, 0)
+        up_mm(11, 0)
+        up_out(10, 1, (0, 1))
         store(10)
         up_mm(11, 1)
         rope_add(11)
         rope_spread(11)
-        latent_out(12)
         rescale(13)
         turn(14)
-        quant_c(12)
-        quant_x(13)
-        latent_mm(13)
-        up_out(11, 0)
-        up_mm(12, 0)
         rope_mul(12)
+        up_out(11, 1, (1,), nc.vector.tensor_copy)
+        quant_x(13)
+        latent_out(12)
+        quant_c(12)
+        latent_mm(13)
         rope_mm(13)
         cast(15)
-        up_out(11, 1, (0, 1))
+        up_out(11, 0)
+        up_mm(12, 0)
+        up_out(11, 1, (0,))
         store(11)
         up_mm(12, 1)
         rope_add(12)
         rope_spread(12)
-        latent_out(13)
         rescale(14)
         turn(15)
-        quant_c(13)
-        quant_x(14)
-        latent_mm(14)
-        up_out(12, 0)
-        up_mm(13, 0)
         rope_mul(13)
+        quant_x(14)
+        latent_out(13)
+        quant_c(13)
+        latent_mm(14)
         rope_mm(14)
         cast(16)
+        up_out(12, 0)
+        up_mm(13, 0)
         up_out(12, 1, (0, 1))
         store(12)
         up_mm(13, 1)
         rope_add(13)
         rope_spread(13)
-        latent_out(14)
         rescale(15)
         turn(16)
-        up_out(13, 1, (1,), nc.vector.tensor_copy)
-        quant_c(14)
-        quant_x(15)
-        latent_mm(15)
-        up_out(13, 0)
-        up_mm(14, 0)
         rope_mul(14)
+        quant_x(15)
+        latent_out(14)
+        quant_c(14)
+        latent_mm(15)
         rope_mm(15)
         cast(17)
-        up_out(13, 1, (0,))
+        up_out(13, 0)
+        up_mm(14, 0)
+        up_out(13, 1, (0, 1))
         store(13)
         up_mm(14, 1)
         rope_add(14)
         rope_spread(14)
-        latent_out(15)
         rescale(16)
         turn(17)
-        quant_c(15)
+        rope_mul(15)
         quant_x(16)
+        latent_out(15)
+        quant_c(15)
         latent_mm(16)
+        rope_mm(16)
+        cast(18)
         up_out(14, 0)
         store(14, 0)
         up_mm(15, 0)
-        rope_mul(15)
-        rope_mm(16)
-        cast(18)
         up_out(14, 1, (0, 1), nc.vector.tensor_copy)
         store(14, 1)
         up_mm(15, 1)
         rope_add(15)
         rope_spread(15)
-        latent_out(16)
         rescale(17)
         turn(18)
-        quant_c(16)
+        rope_mul(16)
         quant_x(17)
+        latent_out(16)
+        quant_c(16)
         latent_mm(17)
+        rope_mm(17)
+        cast(19)
         up_out(15, 0)
         store(15, 0)
         up_mm(16, 0)
-        rope_mul(16)
-        rope_mm(17)
-        cast(19)
         up_out(15, 1, (0, 1), nc.vector.tensor_copy)
         store(15, 1)
         up_mm(16, 1)
-        rope_add(16)
-        rope_spread(16)
-        latent_out(17)

from contextlib import ExitStack

import concourse.mybir as mybir
from concourse.masks import make_identity

FLOPS = 2 * 4096 * 512 * 640 + 2 * 4096 * 512 * 1024

F32 = mybir.dt.float32
BF16 = mybir.dt.bfloat16
U32 = mybir.dt.uint32
U8 = mybir.dt.uint8
FP8 = mybir.dt.float8_e4m3fn
FP8X4 = mybir.dt.float8_e4m3fn_x4
MULT = mybir.AluOpType.mult
ADD = mybir.AluOpType.add

P = 128
STEPS = 16
CAST_ON_SCALAR = (2,)


def tile_multiheadlatentattention_pa_t_kernel(tc, x_bytes, x_scale, cos, sin, wkv_down, w_up, out_0, out_1):
    nc = tc.nc
    x_view = x_bytes.rearrange("b l k -> (b l) k").rearrange("(g p s i) k -> g s p (i k)", p=P, s=2, i=2)
    x_whole = x_bytes.rearrange("b l k -> (b l) k").rearrange("(g p i) k -> p g (i k)", p=P, i=4)
    k_view = out_0.rearrange("b l h d -> (b l) (h d)").rearrange("(g p s i) c -> g s p (i c)", p=P, s=2, i=2)
    v_view = out_1.rearrange("b l h d -> (b l) (h d)").rearrange("(g p s i) c -> g s p (i c)", p=P, s=2, i=2)

    with ExitStack() as ctx:
        keep = ctx.enter_context(tc.tile_pool(name="keep", bufs=1))
        work = ctx.enter_context(tc.tile_pool(name="work", bufs=3))
        psum = ctx.enter_context(tc.psum_pool(name="psum", bufs=1))
        ctx.enter_context(tc.manual_schedule())

        ident = keep.tile([P, P], F32, name="ident")
        scale = keep.tile([P, 4], F32, name="scale")
        w_raw = keep.tile([P, 4, 640], BF16, name="w_raw")
        u_raw = keep.tile([P, 4, 1024], BF16, name="u_raw")
        table = keep.tile([P, 2, 2, 256], BF16, name="table")
        lat_g = keep.tile([P, 2048], BF16, name="lat_g", align_bytes=64)
        rope_g = keep.tile([P, 1024], BF16, name="rope_g", align_bytes=64)
        up_g = [keep.tile([P, 2048], BF16, name="up_g%d" % i, align_bytes=64) for i in range(2)]
        lat_q = keep.tile([P, 512], U32, name="lat_q", align_bytes=64)
        lat_s = keep.tile([P, 512], U8, name="lat_s", align_bytes=64)
        rope_q = keep.tile([P, 256], U32, name="rope_q", align_bytes=64)
        rope_s = keep.tile([P, 256], U8, name="rope_s", align_bytes=64)
        up_q = [keep.tile([P, 512], U32, name="up_q%d" % i, align_bytes=64) for i in range(2)]
        up_s = [keep.tile([P, 512], U8, name="up_s%d" % i, align_bytes=64) for i in range(2)]

        make_identity(nc, ident[:])

        nc.scalar.dma_start(out=scale[:], in_=x_scale.rearrange("a b (p t) -> p (a b t)", t=4))

        x_raw = {}

        def load_x(a, b):
            t = keep.tile([P, b - a, 1024], U8, name="x_raw%d" % a)
            for n in range(a, b):
                x_raw[n] = t[:, n - a, :]
            if b - a == 1:
                nc.sync.dma_start(out=t[:, 0, :], in_=x_view[a // 2, a % 2])
            else:
                nc.sync.dma_start(out=t[:].rearrange("p (g c) k -> p g (c k)", c=2), in_=x_whole[:, a // 2 : b // 2, :])

        load_x(0, 1)
        load_x(1, 2)
        nc.sync.dma_start(out=w_raw[:], in_=wkv_down.rearrange("(p j) c -> p j c", j=4))
        nc.sync.dma_start(out=u_raw[:], in_=w_up.rearrange("(p j) c -> p j c", j=4))
        load_x(2, 4)
        nc.sync.dma_start(out=table[:, 0, :, :], in_=cos.rearrange("(g p i) j -> p g (i j)", p=P, i=4))
        nc.sync.dma_start(out=table[:, 1, :, :], in_=sin.rearrange("(g p i) j -> p g (i j)", p=P, i=4))
        load_x(4, 8)
        load_x(8, 16)

        x_bf, xt, xg, xq, xs, cb, rb, ub, cg, cq, cs, kv, rt = {}, {}, {}, {}, {}, {}, {}, {}, {}, {}, {}, {}, {}

        def ok(n):
            return 0 <= n < STEPS

        def cast(n):
            if not ok(n):
                return
            t = work.tile([P, 1024], BF16, name="x_bf")
            x_bf[n] = t
            src = x_raw[n].bitcast(FP8)
            if n in CAST_ON_SCALAR:
                nc.scalar.copy(out=t[:], in_=src)
            else:
                nc.vector.tensor_copy(out=t[:], in_=src)

        def turn(n):
            if not ok(n):
                return
            t = psum.tile([P, 2, 2, 128], F32, name="xt")
            xt[n] = t
            words = x_bf[n][:].bitcast(F32)
            for i in range(2):
                for u in range(2):
                    nc.tensor.transpose(t[:, u, i, :], words[:, 256 * i + u : 256 * (i + 1) : 2], ident[:])

        def rescale(n):
            if not ok(n):
                return
            t = work.tile([P, 1024], BF16, name="xg", align_bytes=64)
            xg[n] = t
            nc.vector.tensor_tensor(
                out=t[:].rearrange("p (m u e) -> p m u e", u=2, e=2),
                in0=xt[n][:].rearrange("p u i n -> p (u i n)").bitcast(BF16).rearrange("p (u m e) -> p m u e", u=2, e=2),
                in1=scale[:].rearrange("p (u e) -> p u e", e=2).unsqueeze(1).to_broadcast([P, 256, 2, 2]),
                op=MULT,
            )

        def quant(src, width, codes, scales):
            nc.vector.quantize_mx(out=codes.bitcast(FP8X4), scales=scales, in_=src)

        def quant_x(n):
            if not ok(n):
                return
            q = work.tile([P, 256], U32, name="xq", align_bytes=64)
            s = work.tile([P, 256], U8, name="xs", align_bytes=64)
            xq[n], xs[n] = q, s
            quant(xg[n][:], 1024, q[:], s[:])

        def latent_mm(n):
            if not ok(n):
                return
            for i in range(2):
                t = psum.tile([P, 4, 128], F32, name="cb%d" % i)
                cb[n, i] = t
                for j in range(4):
                    nc.tensor.matmul_mx(
                        out=t[:, j, :],
                        lhsT=lat_q[:, 128 * j : 128 * (j + 1)].bitcast(FP8X4),
                        lhsT_scale=lat_s[:, 128 * j : 128 * (j + 1)],
                        rhs=xq[n][:, 128 * i : 128 * (i + 1)].bitcast(FP8X4),
                        rhs_scale=xs[n][:, 128 * i : 128 * (i + 1)],
                        start=True,
                        stop=True,
                    )

        def rope_mm(n):
            if not ok(n):
                return
            t = psum.tile([P, 2, 256], F32, name="rb")
            rb[n] = t
            for i in range(2):
                for a in range(2):
                    nc.tensor.matmul_mx(
                        out=t[:, a, 128 * i : 128 * (i + 1)],
                        lhsT=xq[n][:, 128 * i : 128 * (i + 1)].bitcast(FP8X4),
                        lhsT_scale=xs[n][:, 128 * i : 128 * (i + 1)],
                        rhs=rope_q[:, 128 * a : 128 * (a + 1)].bitcast(FP8X4),
                        rhs_scale=rope_s[:, 128 * a : 128 * (a + 1)],
                        start=True,
                        stop=True,
                    )

        def latent_out(n):
            if not ok(n):
                return
            g = work.tile([P, 1024], BF16, name="cg", align_bytes=64)
            cg[n] = g
            for i in range(2):
                nc.scalar.copy(
                    out=g[:, 512 * i : 512 * (i + 1)].rearrange("p (n t) -> p n t", t=4),
                    in_=cb[n, i][:].rearrange("p t n -> p n t"),
                )

        def quant_c(n):
            if not ok(n):
                return
            q = work.tile([P, 256], U32, name="cq", align_bytes=64)
            s = work.tile([P, 256], U8, name="cs", align_bytes=64)
            cq[n], cs[n] = q, s
            quant(cg[n][:], 1024, q[:], s[:])

        def rope_mul(n):
            if not ok(n):
                return
            t = work.tile([P, 2, 256], F32, name="rt")
            rt[n] = t
            g, s = (n // 2) % 2, n % 2
            nc.vector.tensor_tensor(
                out=t[:].rearrange("p a (m e) -> p a m e", e=2),
                in0=rb[n][:].rearrange("p a (m e) -> p a m e", e=2),
                in1=table[:, :, g, 128 * s : 128 * (s + 1)].unsqueeze(3).to_broadcast([P, 2, 128, 2]),
                op=MULT,
            )

        def kv_tile(n):
            if n not in kv:
                kv[n] = work.tile([P, 2, 2, 4, 192], F32, name="kv", bufs=6)
            return kv[n]

        def rope_add(n):
            if not ok(n):
                return
            t = kv_tile(n)
            nc.vector.tensor_tensor(
                out=t[:, 0, :, 0, 64:192],
                in0=rt[n][:, 0, :].rearrange("p (i c) -> p i c", i=2),
                in1=rt[n][:, 1, :].rearrange("p (i c) -> p i c", i=2),
                op=ADD,
            )

        def rope_spread(n):
            if not ok(n):
                return
            t = kv[n]
            nc.gpsimd.tensor_scalar(
                out=t[:, 0, :, 1:4, 64:192],
                in0=t[:, 0, :, 0, 64:192].unsqueeze(2).to_broadcast([P, 2, 3, 128]),
                scalar1=1.0,
                scalar2=0.0,
                op0=MULT,
                op1=ADD,
            )

        def up_mm(n, i, halves=(0, 1)):
            if not ok(n):
                return
            for half in halves:
                t = psum.tile([P, 512], F32, name="ub%d%d" % (i, half))
                ub[n, i, half] = t
                nc.tensor.matmul_mx(
                    out=t[:],
                    lhsT=cq[n][:, 128 * i : 128 * (i + 1)].bitcast(FP8X4),
                    lhsT_scale=cs[n][:, 128 * i : 128 * (i + 1)],
                    rhs=up_q[half][:].bitcast(FP8X4),
                    rhs_scale=up_s[half][:],
                    start=True,
                    stop=True,
                )

        def up_out(n, i, halves=(0, 1), copy=nc.scalar.copy):
            if not ok(n):
                return
            for half in halves:
                if half == 0:
                    copy(
                        out=kv_tile(n)[:, :, i, :, 0:64].rearrange("p a h c -> p h a c"),
                        in_=ub[n, i, 0][:].rearrange("p (h a c) -> p h a c", h=4, a=2),
                    )
                else:
                    copy(
                        out=kv_tile(n)[:, 1, i, :, 64:192],
                        in_=ub[n, i, 1][:].rearrange("p (h c) -> p h c", h=4),
                    )

        def store_part(n, i, part):
            if not ok(n):
                return
            g, s = n // 2, n % 2
            view = k_view if part == 0 else v_view
            nc.sync.dma_start(out=view[g, s][:, 768 * i : 768 * (i + 1)], in_=kv[n][:, part, i].rearrange("p h d -> p (h d)"))

        def store(n, i=None):
            if not ok(n):
                return
            g, s = n // 2, n % 2
            a, b = (0, 2) if i is None else (i, i + 1)
            for once in range(1):
                nc.sync.dma_start(out=v_view[g, s][:, 768 * a : 768 * b], in_=kv[n][:, 1, a:b].rearrange("p i h d -> p (i h d)"))
                nc.sync.dma_start(out=k_view[g, s][:, 768 * a : 768 * b], in_=kv[n][:, 0, a:b].rearrange("p i h d -> p (i h d)"))

        lat_out_view = lat_g[:].rearrange("p (t m j) -> p t m j", t=4, j=4)
        lat_in_view = w_raw[:, :, 0:512].rearrange("p j (m t) -> p t m j", t=4)
        rope_out_view = rope_g[:].rearrange("p (a c j) -> p a c j", a=2, j=4)
        rope_in_view = w_raw[:, :, 512:640].rearrange("p j c -> p c j")
        up_in_view = u_raw[:].rearrange("p j (h f c) -> p f h c j", h=4, f=2)

        def lat_copy(a, b, copy):
            copy(out=lat_out_view[:, a:b], in_=lat_in_view[:, a:b])

        def rope_copy(kind):
            if kind == 0:
                nc.scalar.copy(out=rope_out_view[:, 0], in_=rope_in_view)
            elif kind == 1:
                nc.scalar.copy(out=rope_out_view[:, 1, 1::2], in_=rope_in_view[:, 0::2])
            else:
                nc.vector.tensor_scalar(out=rope_out_view[:, 1, 0::2], in0=rope_in_view[:, 1::2], scalar1=-1.0, scalar2=None, op0=MULT)

        def quant_lat():
            quant(lat_g[:], 2048, lat_q[:], lat_s[:])

        def quant_rope():
            quant(rope_g[:], 1024, rope_q[:], rope_s[:])

        def quant_up(f):
            quant(up_g[f][:], 2048, up_q[f][:], up_s[f][:])

        def up_group(f, h, h_end, copy):
            copy(
                out=up_g[f][:].rearrange("p (h c j) -> p h c j", h=4, j=4)[:, h:h_end],
                in_=up_in_view[:, f, h:h_end],
            )

        cast(0)
        rope_copy(1)
        cast(1)
        rope_copy(2)
        rope_copy(0)
        lat_copy(1, 4, nc.scalar.copy)
        turn(0)
        rescale(0)
        lat_copy(0, 1, nc.vector.tensor_copy)
        quant_rope()
        quant_x(0)
        turn(1)
        cast(2)
        up_group(1, 2, 4, nc.vector.tensor_copy)
        up_group(1, 0, 2, nc.scalar.copy)
        rescale(1)
        quant_lat()
        quant_x(1)
        rope_mm(0)
        latent_mm(0)
        turn(2)
        up_group(0, 0, 4, nc.vector.tensor_copy)
        rope_mul(0)
        latent_out(0)
        quant_up(0)
        quant_c(0)
        latent_mm(1)
        cast(3)
        latent_out(1)
        up_mm(0, 1, (0,))
        up_mm(0, 0, (0,))
        quant_up(1)
        up_out(0, 0, (0,))
        rope_mm(1)
        up_mm(0, 0, (1,))
        up_out(0, 0, (1,))
        rescale(2)
        turn(3)
        up_out(0, 1, (0,))
        rope_mul(1)
        rope_add(0)
        up_mm(0, 1, (1,))
        quant_c(1)
        up_out(0, 1, (1,))
        quant_x(2)
        latent_mm(2)
        cast(4)
        store_part(0, 0, 1)
        store_part(0, 1, 1)
        rope_mm(2)
        latent_out(2)
        rope_add(1)
        rope_spread(0)
        store_part(0, 0, 0)
        up_mm(1, 1)
        up_mm(1, 0)
        up_out(1, 1, (0, 1))
        rescale(3)
        rope_mul(2)
        turn(4)
        quant_c(2)
        store_part(0, 1, 0)
        rope_add(2)
        up_out(1, 0)
        quant_x(3)
        rescale(4)
        store_part(1, 1, 1)
        rope_spread(1)
        up_mm(2, 1)
        cast(5)
        store_part(1, 0, 0)
        latent_mm(3)
        up_mm(2, 0)
        rope_mm(3)
        store_part(1, 1, 0)
        turn(5)
        store_part(1, 0, 1)
        rope_spread(2)
        up_out(2, 1, (1,), nc.vector.tensor_copy)
        rope_mul(3)
        quant_x(4)
        latent_out(3)
        quant_c(3)
        latent_mm(4)
        rope_mm(4)
        cast(6)
        up_out(2, 0)
        up_mm(3, 0)
        up_out(2, 1, (0,))
        store(2)
        up_mm(3, 1)
        rope_add(3)
        rope_spread(3)
        rescale(5)
        turn(6)
        rope_mul(4)
        quant_x(5)
        latent_out(4)
        quant_c(4)
        latent_mm(5)
        rope_mm(5)
        cast(7)
        up_out(3, 0)
        up_mm(4, 0)
        up_out(3, 1, (0, 1))
        store(3)
        up_mm(4, 1)
        rope_add(4)
        rope_spread(4)
        rescale(6)
        turn(7)
        rope_mul(5)
        quant_x(6)
        latent_out(5)
        quant_c(5)
        latent_mm(6)
        rope_mm(6)
        cast(8)
        up_out(4, 0)
        up_mm(5, 0)
        up_out(4, 1, (0, 1))
        store(4)
        up_mm(5, 1)
        rope_add(5)
        rope_spread(5)
        rescale(7)
        turn(8)
        rope_mul(6)
        up_out(5, 1, (1,), nc.vector.tensor_copy)
        quant_x(7)
        latent_out(6)
        quant_c(6)
        latent_mm(7)
        rope_mm(7)
        cast(9)
        up_out(5, 0)
        up_mm(6, 0)
        up_out(5, 1, (0,))
        store(5)
        up_mm(6, 1)
        rope_add(6)
        rope_spread(6)
        rescale(8)
        turn(9)
        rope_mul(7)
        quant_x(8)
        latent_out(7)
        quant_c(7)
        latent_mm(8)
        rope_mm(8)
        cast(10)
        up_out(6, 0)
        up_mm(7, 0)
        up_out(6, 1, (0, 1))
        store(6)
        up_mm(7, 1)
        rope_add(7)
        rope_spread(7)
        rescale(9)
        turn(10)
        rope_mul(8)
        quant_x(9)
        latent_out(8)
        quant_c(8)
        latent_mm(9)
        rope_mm(9)
        cast(11)
        up_out(7, 0)
        up_mm(8, 0)
        up_out(7, 1, (0, 1))
        store(7)
        up_mm(8, 1)
        rope_add(8)
        rope_spread(8)
        rescale(10)
        turn(11)
        rope_mul(9)
        up_out(8, 1, (1,), nc.vector.tensor_copy)
        quant_x(10)
        latent_out(9)
        quant_c(9)
        latent_mm(10)
        rope_mm(10)
        cast(12)
        up_out(8, 0)
        up_mm(9, 0)
        up_out(8, 1, (0,))
        store(8)
        up_mm(9, 1)
        rope_add(9)
        rope_spread(9)
        rescale(11)
        turn(12)
        rope_mul(10)
        quant_x(11)
        latent_out(10)
        quant_c(10)
        latent_mm(11)
        rope_mm(11)
        cast(13)
        up_out(9, 0)
        up_mm(10, 0)
        up_out(9, 1, (0, 1))
        store(9)
        up_mm(10, 1)
        rope_add(10)
        rope_spread(10)
        rescale(12)
        turn(13)
        rope_mul(11)
        quant_x(12)
        latent_out(11)
        quant_c(11)
        latent_mm(12)
        rope_mm(12)
        cast(14)
        up_out(10, 0)
        up_mm(11, 0)
        up_out(10, 1, (0, 1))
        store(10)
        up_mm(11, 1)
        rope_add(11)
        rope_spread(11)
        rescale(13)
        turn(14)
        rope_mul(12)
        up_out(11, 1, (1,), nc.vector.tensor_copy)
        quant_x(13)
        latent_out(12)
        quant_c(12)
        latent_mm(13)
        rope_mm(13)
        cast(15)
        up_out(11, 0)
        up_mm(12, 0)
        up_out(11, 1, (0,))
        store(11)
        up_mm(12, 1)
        rope_add(12)
        rope_spread(12)
        rescale(14)
        turn(15)
        rope_mul(13)
        quant_x(14)
        latent_out(13)
        quant_c(13)
        latent_mm(14)
        rope_mm(14)
        cast(16)
        up_out(12, 0)
        up_mm(13, 0)
        up_out(12, 1, (0, 1))
        store(12)
        up_mm(13, 1)
        rope_add(13)
        rope_spread(13)
        rescale(15)
        turn(16)
        rope_mul(14)
        quant_x(15)
        latent_out(14)
        quant_c(14)
        latent_mm(15)
        rope_mm(15)
        cast(17)
        up_out(13, 0)
        up_mm(14, 0)
        up_out(13, 1, (0, 1))
        store(13)
        up_mm(14, 1)
        rope_add(14)
        rope_spread(14)
        rescale(16)
        turn(17)
        rope_mul(15)
        quant_x(16)
        latent_out(15)
        quant_c(15)
        latent_mm(16)
        rope_mm(16)
        cast(18)
        up_out(14, 0)
        store(14, 0)
        up_mm(15, 0)
        up_out(14, 1, (0, 1), nc.vector.tensor_copy)
        store(14, 1)
        up_mm(15, 1)
        rope_add(15)
        rope_spread(15)
        rescale(17)
        turn(18)
        rope_mul(16)
        quant_x(17)
        latent_out(16)
        quant_c(16)
        latent_mm(17)
        rope_mm(17)
        cast(19)
        up_out(15, 0)
        store(15, 0)
        up_mm(16, 0)
        up_out(15, 1, (0, 1), nc.vector.tensor_copy)
        store(15, 1)
        up_mm(16, 1)
